import numpy as np
import ml_dtypes


def mxq(x, axis, fmt="e4m3"):
    dtype, down = {"e4m3": (ml_dtypes.float8_e4m3fn, 7), "e5m2": (ml_dtypes.float8_e5m2, 14)}[fmt]
    v = np.moveaxis(np.asarray(x, np.float32).astype(ml_dtypes.bfloat16).astype(np.float64), axis, -1)
    blocks = v.reshape(v.shape[:-1] + (-1, 32))
    amax = np.abs(blocks).max(-1, keepdims=True)
    byte = np.maximum(np.where(amax > 0, np.frexp(amax)[1] - 1 + 127, 0) - down, 1)
    scale = np.exp2(byte - 127.0)
    codes = (blocks / scale).astype(np.float32).astype(dtype).astype(np.float64)
    return np.moveaxis((codes * scale).reshape(v.shape), -1, axis)


WIDE = False


def mx_kscale(k):
    if not WIDE:
        return np.ones(k)
    levels = np.array([20, -20, 10, -10, 0])
    a = np.random.permutation(np.resize(levels, k // 512 * 4)).reshape(k // 512, 4)
    idx = np.arange(k)
    return np.exp2(a[idx // 512, idx % 128 // 32])


BF16 = ml_dtypes.bfloat16


def bf(x):
    return np.asarray(x, np.float32).astype(BF16)


def f64(x):
    return np.asarray(x).astype(np.float64)


B, C, H, D, N, CO = 4, 128, 2048, 512, 4, 512
NC = N * C
EPS = 1e-5
GS = 8.0


def stack_heads(head_res):
    return head_res.transpose(1, 0, 2, 3).reshape(B, NC, D)


def setup_inputs():
    u = mx_kscale(CO)
    head = np.maximum(np.random.standard_normal((N, B, C, D)), 0.0) + 0.25 * np.random.standard_normal((N, B, C, D))
    head_res = bf(head)
    W0 = bf(np.random.standard_normal((CO, NC)) / np.sqrt(NC))
    g_m = bf(1.0 + 0.1 * np.random.standard_normal(CO))
    b_m = bf(0.1 * np.random.standard_normal(CO))
    g = bf(np.random.standard_normal((B, CO, D)) * np.exp2(np.random.randint(-12, 1, (B, 1, D))) * GS * u[None, :, None])
    m = f64(W0)[None] @ stack_heads(f64(head_res))
    mean = m.mean(axis=(0, 2), keepdims=True)
    var = m.var(axis=(0, 2), keepdims=True)
    r = 1.0 / np.sqrt(var + EPS)
    xh = (m - mean) * r
    yy = np.maximum(xh * f64(g_m)[None, :, None] + f64(b_m)[None, :, None], 0.0)
    return {'head_res': head_res,
            'W_merge': bf(f64(W0) / u[:, None]),
            'g_m': g_m,
            'b_m': b_m,
            'xhat': np.asarray(xh, np.float32),
            'rstd': np.asarray(r.reshape(CO), np.float32),
            'y': np.asarray(yy, np.float32),
            'grad_out': g}


def reference(head_res, W_merge, g_m, b_m, xhat, rstd, y, grad_out):
    xh = f64(xhat)
    dy = f64(grad_out) * (f64(y) > 0.0)
    s1 = dy.mean(axis=(0, 2), keepdims=True)
    s2 = (dy * xh).mean(axis=(0, 2), keepdims=True)
    dm = (f64(g_m) * f64(rstd))[None, :, None] * (dy - s1 - xh * s2)
    dcat = mxq(f64(W_merge), 0, 'e4m3').T[None] @ mxq(dm, 1, 'e5m2')
    return dcat.reshape(B, N, C, D).transpose(1, 0, 2, 3)

@@ -1,0 +1,161 @@
+from contextlib import ExitStack
+
+import concourse.mybir as mybir
+
+F32 = mybir.dt.float32
+BF16 = mybir.dt.bfloat16
+U32 = mybir.dt.uint32
+U8 = mybir.dt.uint8
+E4M3X4 = mybir.dt.float8_e4m3fn_x4
+E5M2X4 = mybir.dt.float8_e5m2_x4
+ALU = mybir.AluOpType
+ACT = mybir.ActivationFunctionType
+
+P = 128
+PACK = 4
+B = 4
+D = 512
+HEADS = 4
+CO = P * PACK
+NC = HEADS * P
+TOKENS = B * D
+RUN = 4
+
+FLOPS = 2 * CO * NC * TOKENS
+BYTES = 3 * 4 * CO * TOKENS + 2 * CO * TOKENS + 2 * CO * NC + 6 * CO
+
+
+def regrouped(planar, grouped):
+    return (
+        planar.rearrange("p j (c i) -> p c j i", i=RUN),
+        grouped.rearrange("p (c i) j -> p c j i", i=RUN),
+    )
+
+
+def tile_block_height_reducing_filtering_pb_v_kernel(
+    tc, head_res, W_merge, g_m, b_m, xhat, rstd, y, grad_out, out
+):
+    nc = tc.nc
+    with ExitStack() as ctx:
+        keep = ctx.enter_context(tc.tile_pool(name="keep", bufs=1))
+        ring = ctx.enter_context(tc.tile_pool(name="ring", bufs=2))
+        psum = ctx.enter_context(tc.psum_pool(name="psum", bufs=8))
+
+        gain_bf = keep.tile([P, PACK], BF16, name="gain_bf")
+        inv_std = keep.tile([P, PACK], F32, name="inv_std")
+        nc.scalar.dma_start(out=gain_bf[:], in_=g_m.rearrange("(p j) -> p j", j=PACK))
+        nc.scalar.dma_start(out=inv_std[:], in_=rstd.rearrange("(p j) -> p j", j=PACK))
+
+        g_slots = grad_out.rearrange("b (p j) d -> j p b d", j=PACK)
+        y_slots = y.rearrange("b (p j) d -> j p b d", j=PACK)
+        x_slots = xhat.rearrange("b (p j) d -> j p b d", j=PACK)
+        g_sb = [keep.tile([P, B, D], BF16, name="g%d" % j) for j in range(PACK)]
+        x_sb = [keep.tile([P, B, D], F32, name="x%d" % j) for j in range(PACK)]
+        y_sb = {}
+        w_raw = keep.tile([P, PACK, NC], BF16, name="w_raw")
+
+        def load(j):
+            if j < PACK:
+                y_sb[j] = ring.tile([P, B, D], F32, name="y")
+                nc.sync.dma_start(out=g_sb[j][:], in_=g_slots[j])
+                nc.sync.dma_start(out=y_sb[j][:], in_=y_slots[j])
+                nc.sync.dma_start(out=x_sb[j][:], in_=x_slots[j])
+            elif j == PACK:
+                nc.sync.dma_start(out=w_raw[:], in_=W_merge.rearrange("(p j) c -> p j c", j=PACK))
+
+        load(0)
+        load(1)
+
+        gain = keep.tile([P, PACK], F32, name="gain")
+        neg_rstd_mean = keep.tile([P, PACK], F32, name="neg_rstd_mean")
+        nc.vector.tensor_copy(out=gain[:], in_=gain_bf[:])
+        nc.vector.tensor_scalar_mul(out=neg_rstd_mean[:], in0=inv_std[:], scalar1=-1.0 / TOKENS)
+
+        sum_m = keep.tile([P, PACK], F32, name="sum_m")
+        neg_a_s1 = keep.tile([P, PACK], F32, name="neg_a_s1")
+        neg_a_s2 = keep.tile([P, PACK], F32, name="neg_a_s2")
+        m_sb = [keep.tile([P, B, D], F32, name="m%d" % j) for j in range(PACK)]
+        shifted = {}
+        dm_planar = keep.tile([P, B, PACK, D], BF16, name="dm_planar")
+
+        def mask_and_shift(j):
+            slot = slice(j, j + 1)
+            scaled_g = ring.tile([P, B, D], F32, name="scaled_g")
+            nc.scalar.mul(out=scaled_g[:], in_=g_sb[j][:], mul=gain[:, slot])
+            nc.vector.scalar_tensor_tensor(
+                out=m_sb[j][:], in0=y_sb[j][:], scalar=0.0, in1=scaled_g[:],
+                op0=ALU.is_gt, op1=ALU.mult, accum_out=sum_m[:, slot],
+            )
+            load(j + 2)
+            nc.scalar.mul(out=neg_a_s1[:, slot], in_=sum_m[:, slot], mul=neg_rstd_mean[:, slot])
+            shifted[j] = ring.tile([P, B, D], F32, name="shifted")
+            nc.scalar.activation(
+                out=shifted[j][:], in_=m_sb[j][:], func=ACT.Identity,
+                bias=neg_a_s1[:, slot], scale=inv_std[:, slot],
+            )
+
+        def second_mean(j):
+            slot = slice(j, j + 1)
+            products = keep.tile([P, B, D], F32, name="products")
+            nc.vector.scalar_tensor_tensor(
+                out=products[:], in0=m_sb[j][:], scalar=neg_rstd_mean[:, slot], in1=x_sb[j][:],
+                op0=ALU.mult, op1=ALU.mult, accum_out=neg_a_s2[:, slot],
+            )
+
+        def finish_dm(j, samples):
+            nc.vector.scalar_tensor_tensor(
+                out=dm_planar[:, samples, j, :], in0=x_sb[j][:, samples, :],
+                scalar=neg_a_s2[:, j : j + 1], in1=shifted[j][:, samples, :],
+                op0=ALU.mult, op1=ALU.add,
+            )
+
+        every_sample = slice(0, B)
+        last = PACK - 1
+        mask_and_shift(0)
+        second_mean(0)
+        for j in range(1, PACK):
+            mask_and_shift(j)
+            finish_dm(j - 1, every_sample)
+            second_mean(j)
+
+        w_grouped = keep.tile([P, NC, PACK], BF16, name="w_grouped", align_bytes=64)
+        w_codes = keep.tile([P, NC], U32, name="w_codes", align_bytes=64)
+        w_scales = keep.tile([P, NC], U8, name="w_scales", align_bytes=64)
+        w_from, w_to = regrouped(w_raw[:], w_grouped[:])
+        nc.scalar.copy(out=w_to, in_=w_from)
+        nc.vector.quantize_mx(
+            out=w_codes[:].bitcast(E4M3X4), scales=w_scales[:],
+            in_=w_grouped[:].rearrange("p c j -> p (c j)"),
+        )
+
+        dm_grouped = [
+            keep.tile([P, D, PACK], BF16, name="dm_grouped%d" % b, align_bytes=64) for b in range(B)
+        ]
+        dm_codes = keep.tile([P, B, D], U32, name="dm_codes", align_bytes=64)
+        dm_scales = keep.tile([P, B, D], U8, name="dm_scales", align_bytes=64)
+
+        finish_dm(last, slice(0, 1))
+        for b in range(B):
+            dm_from, dm_to = regrouped(dm_planar[:, b], dm_grouped[b][:])
+            nc.vector.tensor_copy(out=dm_to, in_=dm_from)
+            if b + 1 < B:
+                finish_dm(last, slice(b + 1, b + 2))
+            nc.vector.quantize_mx(
+                out=dm_codes[:, b, :].bitcast(E5M2X4), scales=dm_scales[:, b, :],
+                in_=dm_grouped[b][:].rearrange("p d j -> p (d j)"),
+            )
+            result = ring.tile([P, HEADS, D], F32, name="result")
+            for n in range(HEADS):
+                head = slice(n * P, (n + 1) * P)
+                acc = psum.tile([P, D], F32, name="acc")
+                nc.tensor.matmul_mx(
+                    out=acc[:],
+                    lhsT=w_codes[:, head].bitcast(E4M3X4), lhsT_scale=w_scales[:, head],
+                    rhs=dm_codes[:, b, :].bitcast(E5M2X4), rhs_scale=dm_scales[:, b, :],
+                    start=True, stop=True,
+                )
+                if b == B - 1 and n % 2 == 1:
+                    nc.vector.tensor_copy(out=result[:, n, :], in_=acc[:])
+                else:
+                    nc.scalar.copy(out=result[:, n, :], in_=acc[:])
+                nc.sync.dma_start(out=out[n, b], in_=result[:, n, :])

@@ -50,55 +50,47 @@ def tile_block_height_reducing_filtering_pb_v_kernel(
         y_slots = y.rearrange("b (p j) d -> j p b d", j=PACK)
         x_slots = xhat.rearrange("b (p j) d -> j p b d", j=PACK)
         g_sb = [keep.tile([P, B, D], BF16, name="g%d" % j) for j in range(PACK)]
+        y_sb = [keep.tile([P, B, D], F32, name="y%d" % j) for j in range(PACK)]
         x_sb = [keep.tile([P, B, D], F32, name="x%d" % j) for j in range(PACK)]
-        y_sb = {}
         w_raw = keep.tile([P, PACK, NC], BF16, name="w_raw")
-
-        def load(j):
-            if j < PACK:
-                y_sb[j] = ring.tile([P, B, D], F32, name="y")
-                nc.sync.dma_start(out=g_sb[j][:], in_=g_slots[j])
-                nc.sync.dma_start(out=y_sb[j][:], in_=y_slots[j])
-                nc.sync.dma_start(out=x_sb[j][:], in_=x_slots[j])
-            elif j == PACK:
-                nc.sync.dma_start(out=w_raw[:], in_=W_merge.rearrange("(p j) c -> p j c", j=PACK))
-
-        load(0)
-        load(1)
+        for j in range(PACK):
+            nc.sync.dma_start(out=g_sb[j][:], in_=g_slots[j])
+            nc.sync.dma_start(out=y_sb[j][:], in_=y_slots[j])
+            nc.sync.dma_start(out=x_sb[j][:], in_=x_slots[j])
+        nc.sync.dma_start(out=w_raw[:], in_=W_merge.rearrange("(p j) c -> p j c", j=PACK))
 
         gain = keep.tile([P, PACK], F32, name="gain")
-        neg_rstd_mean = keep.tile([P, PACK], F32, name="neg_rstd_mean")
+        a_fac = keep.tile([P, PACK], F32, name="a_fac")
+        neg_a_mean = keep.tile([P, PACK], F32, name="neg_a_mean")
         nc.vector.tensor_copy(out=gain[:], in_=gain_bf[:])
-        nc.vector.tensor_scalar_mul(out=neg_rstd_mean[:], in0=inv_std[:], scalar1=-1.0 / TOKENS)
+        nc.vector.tensor_mul(out=a_fac[:], in0=gain[:], in1=inv_std[:])
+        nc.vector.tensor_scalar_mul(out=neg_a_mean[:], in0=a_fac[:], scalar1=-1.0 / TOKENS)
 
-        sum_m = keep.tile([P, PACK], F32, name="sum_m")
+        sum_dy = keep.tile([P, PACK], F32, name="sum_dy")
         neg_a_s1 = keep.tile([P, PACK], F32, name="neg_a_s1")
         neg_a_s2 = keep.tile([P, PACK], F32, name="neg_a_s2")
-        m_sb = [keep.tile([P, B, D], F32, name="m%d" % j) for j in range(PACK)]
+        dy_sb = [keep.tile([P, B, D], BF16, name="dy%d" % j) for j in range(PACK)]
         shifted = {}
         dm_planar = keep.tile([P, B, PACK, D], BF16, name="dm_planar")
 
         def mask_and_shift(j):
             slot = slice(j, j + 1)
-            scaled_g = ring.tile([P, B, D], F32, name="scaled_g")
-            nc.scalar.mul(out=scaled_g[:], in_=g_sb[j][:], mul=gain[:, slot])
             nc.vector.scalar_tensor_tensor(
-                out=m_sb[j][:], in0=y_sb[j][:], scalar=0.0, in1=scaled_g[:],
-                op0=ALU.is_gt, op1=ALU.mult, accum_out=sum_m[:, slot],
+                out=dy_sb[j][:], in0=y_sb[j][:], scalar=0.0, in1=g_sb[j][:],
+                op0=ALU.is_gt, op1=ALU.mult, accum_out=sum_dy[:, slot],
             )
-            load(j + 2)
-            nc.scalar.mul(out=neg_a_s1[:, slot], in_=sum_m[:, slot], mul=neg_rstd_mean[:, slot])
+            nc.scalar.mul(out=neg_a_s1[:, slot], in_=sum_dy[:, slot], mul=neg_a_mean[:, slot])
             shifted[j] = ring.tile([P, B, D], F32, name="shifted")
             nc.scalar.activation(
-                out=shifted[j][:], in_=m_sb[j][:], func=ACT.Identity,
-                bias=neg_a_s1[:, slot], scale=inv_std[:, slot],
+                out=shifted[j][:], in_=dy_sb[j][:], func=ACT.Identity,
+                bias=neg_a_s1[:, slot], scale=a_fac[:, slot],
             )
 
         def second_mean(j):
             slot = slice(j, j + 1)
-            products = keep.tile([P, B, D], F32, name="products")
+            products = keep.tile([P, B, D], BF16, name="products")
             nc.vector.scalar_tensor_tensor(
-                out=products[:], in0=m_sb[j][:], scalar=neg_rstd_mean[:, slot], in1=x_sb[j][:],
+                out=products[:], in0=dy_sb[j][:], scalar=neg_a_mean[:, slot], in1=x_sb[j][:],
                 op0=ALU.mult, op1=ALU.mult, accum_out=neg_a_s2[:, slot],
             )
 

@@ -10,6 +10,7 @@ E4M3X4 = mybir.dt.float8_e4m3fn_x4
 E5M2X4 = mybir.dt.float8_e5m2_x4
 ALU = mybir.AluOpType
 ACT = mybir.ActivationFunctionType
+AX = mybir.AxisListType
 
 P = 128
 PACK = 4
@@ -24,12 +25,27 @@ RUN = 4
 FLOPS = 2 * CO * NC * TOKENS
 BYTES = 3 * 4 * CO * TOKENS + 2 * CO * TOKENS + 2 * CO * NC + 6 * CO
 
+MASK_PARTS = {0: 4, 1: 1, 2: 1, 3: 1}
+PROD_PARTS = {0: 4, 1: 1, 2: 1, 3: 1}
+SIGN_SLOTS = (2,)
+PAIRS = False
+W_AFTER = 'end'
+V_EVAC = ((3, 1), (3, 3))
+ACT_REGROUP = ()
+RESULT_BUFS = 2
+SHIFT_BUFS = 2
+
 
 def regrouped(planar, grouped):
     return (
         planar.rearrange("p j (c i) -> p c j i", i=RUN),
         grouped.rearrange("p (c i) j -> p c j i", i=RUN),
     )
+
+
+def pieces(n):
+    step = B // n
+    return [slice(k * step, (k + 1) * step) for k in range(n)]
 
 
 def tile_block_height_reducing_filtering_pb_v_kernel(
@@ -39,6 +55,8 @@ def tile_block_height_reducing_filtering_pb_v_kernel(
     with ExitStack() as ctx:
         keep = ctx.enter_context(tc.tile_pool(name="keep", bufs=1))
         ring = ctx.enter_context(tc.tile_pool(name="ring", bufs=2))
+        shift_pool = ctx.enter_context(tc.tile_pool(name="shift_pool", bufs=SHIFT_BUFS))
+        res_pool = ctx.enter_context(tc.tile_pool(name="res_pool", bufs=RESULT_BUFS))
         psum = ctx.enter_context(tc.psum_pool(name="psum", bufs=8))
 
         gain_bf = keep.tile([P, PACK], BF16, name="gain_bf")
@@ -53,11 +71,28 @@ def tile_block_height_reducing_filtering_pb_v_kernel(
         y_sb = [keep.tile([P, B, D], F32, name="y%d" % j) for j in range(PACK)]
         x_sb = [keep.tile([P, B, D], F32, name="x%d" % j) for j in range(PACK)]
         w_raw = keep.tile([P, PACK, NC], BF16, name="w_raw")
+
+        def load_w():
+            nc.sync.dma_start(out=w_raw[:], in_=W_merge.rearrange("(p j) c -> p j c", j=PACK))
+
+        if W_AFTER == "start":
+            load_w()
         for j in range(PACK):
-            nc.sync.dma_start(out=g_sb[j][:], in_=g_slots[j])
-            nc.sync.dma_start(out=y_sb[j][:], in_=y_slots[j])
-            nc.sync.dma_start(out=x_sb[j][:], in_=x_slots[j])
-        nc.sync.dma_start(out=w_raw[:], in_=W_merge.rearrange("(p j) c -> p j c", j=PACK))
+            for s in pieces(MASK_PARTS[j]):
+                if j in SIGN_SLOTS:
+                    nc.sync.dma_start(out=y_sb[j][:, s, :], in_=y_slots[j][:, s, :])
+                    nc.sync.dma_start(out=g_sb[j][:, s, :], in_=g_slots[j][:, s, :])
+                else:
+                    nc.sync.dma_start(out=g_sb[j][:, s, :], in_=g_slots[j][:, s, :])
+                    nc.sync.dma_start(out=y_sb[j][:, s, :], in_=y_slots[j][:, s, :])
+            if W_AFTER == ("y", j):
+                load_w()
+            for s in pieces(PROD_PARTS[j]):
+                nc.sync.dma_start(out=x_sb[j][:, s, :], in_=x_slots[j][:, s, :])
+            if W_AFTER == ("x", j):
+                load_w()
+        if W_AFTER == "end":
+            load_w()
 
         gain = keep.tile([P, PACK], F32, name="gain")
         a_fac = keep.tile([P, PACK], F32, name="a_fac")
@@ -66,21 +101,45 @@ def tile_block_height_reducing_filtering_pb_v_kernel(
         nc.vector.tensor_mul(out=a_fac[:], in0=gain[:], in1=inv_std[:])
         nc.vector.tensor_scalar_mul(out=neg_a_mean[:], in0=a_fac[:], scalar1=-1.0 / TOKENS)
 
-        sum_dy = keep.tile([P, PACK], F32, name="sum_dy")
+        sum_parts = keep.tile([P, PACK, B], F32, name="sum_parts")
+        s2_parts = keep.tile([P, PACK, B], F32, name="s2_parts")
+        small_junk = keep.tile([P, PACK, B], F32, name="small_junk")
         neg_a_s1 = keep.tile([P, PACK], F32, name="neg_a_s1")
         neg_a_s2 = keep.tile([P, PACK], F32, name="neg_a_s2")
         dy_sb = [keep.tile([P, B, D], BF16, name="dy%d" % j) for j in range(PACK)]
         shifted = {}
-        dm_planar = keep.tile([P, B, PACK, D], BF16, name="dm_planar")
+        dm_planar = keep.tile([P, PACK, B, D], BF16, name="dm_planar")
+        dm_grouped = keep.tile([P, B, D, PACK], BF16, name="dm_grouped", align_bytes=64)
 
         def mask_and_shift(j):
             slot = slice(j, j + 1)
-            nc.vector.scalar_tensor_tensor(
-                out=dy_sb[j][:], in0=y_sb[j][:], scalar=0.0, in1=g_sb[j][:],
-                op0=ALU.is_gt, op1=ALU.mult, accum_out=sum_dy[:, slot],
-            )
-            nc.scalar.mul(out=neg_a_s1[:, slot], in_=sum_dy[:, slot], mul=neg_a_mean[:, slot])
-            shifted[j] = ring.tile([P, B, D], F32, name="shifted")
+            n = MASK_PARTS[j]
+            if j in SIGN_SLOTS:
+                for s in pieces(n):
+                    relu_mask = ring.tile([P, B, D], BF16, name="relu_mask")
+                    nc.scalar.activation(out=relu_mask[:, s, :], in_=y_sb[j][:, s, :], func=ACT.Sign)
+                    nc.vector.tensor_tensor(
+                        out=dy_sb[j][:, s, :], in0=relu_mask[:, s, :], in1=g_sb[j][:, s, :], op=ALU.mult
+                    )
+                big_junk = keep.tile([P, B, D], BF16, name="big_junk")
+                nc.scalar.activation(
+                    out=big_junk[:], in_=dy_sb[j][:], func=ACT.Copy,
+                    scale=neg_a_mean[:, slot], accum_out=neg_a_s1[:, slot],
+                )
+            else:
+                for k, s in enumerate(pieces(n)):
+                    nc.vector.scalar_tensor_tensor(
+                        out=dy_sb[j][:, s, :], in0=y_sb[j][:, s, :], scalar=0.0, in1=g_sb[j][:, s, :],
+                        op0=ALU.is_gt, op1=ALU.mult, accum_out=sum_parts[:, j, k : k + 1],
+                    )
+                if n == 1:
+                    nc.scalar.mul(out=neg_a_s1[:, slot], in_=sum_parts[:, j, 0:1], mul=neg_a_mean[:, slot])
+                else:
+                    nc.scalar.activation(
+                        out=small_junk[:, j, 0:n], in_=sum_parts[:, j, 0:n], func=ACT.Copy,
+                        scale=neg_a_mean[:, slot], accum_out=neg_a_s1[:, slot],
+                    )
+            shifted[j] = shift_pool.tile([P, B, D], F32, name="shifted")
             nc.scalar.activation(
                 out=shifted[j][:], in_=dy_sb[j][:], func=ACT.Identity,
                 bias=neg_a_s1[:, slot], scale=a_fac[:, slot],
@@ -88,17 +147,28 @@ def tile_block_height_reducing_filtering_pb_v_kernel(
 
         def second_mean(j):
             slot = slice(j, j + 1)
+            n = PROD_PARTS[j]
             products = keep.tile([P, B, D], BF16, name="products")
-            nc.vector.scalar_tensor_tensor(
-                out=products[:], in0=dy_sb[j][:], scalar=neg_a_mean[:, slot], in1=x_sb[j][:],
-                op0=ALU.mult, op1=ALU.mult, accum_out=neg_a_s2[:, slot],
-            )
+            for k, s in enumerate(pieces(n)):
+                nc.vector.scalar_tensor_tensor(
+                    out=products[:, s, :], in0=dy_sb[j][:, s, :], scalar=neg_a_mean[:, slot],
+                    in1=x_sb[j][:, s, :], op0=ALU.mult, op1=ALU.mult,
+                    accum_out=(neg_a_s2[:, slot] if n == 1 else s2_parts[:, j, k : k + 1]),
+                )
+            if n > 1:
+                nc.vector.tensor_reduce(out=neg_a_s2[:, slot], in_=s2_parts[:, j, 0:n], axis=AX.X, op=ALU.add)
 
         def finish_dm(j, samples):
             nc.vector.scalar_tensor_tensor(
-                out=dm_planar[:, samples, j, :], in0=x_sb[j][:, samples, :],
+                out=dm_planar[:, j, samples, :], in0=x_sb[j][:, samples, :],
                 scalar=neg_a_s2[:, j : j + 1], in1=shifted[j][:, samples, :],
                 op0=ALU.mult, op1=ALU.add,
+            )
+
+        def lay_pair(engine_copy, first, b):
+            engine_copy(
+                out=dm_grouped[:, b, :, first : first + 2],
+                in_=dm_planar[:, first : first + 2, b, :].rearrange("p j d -> p d j"),
             )
 
         every_sample = slice(0, B)
@@ -108,6 +178,9 @@ def tile_block_height_reducing_filtering_pb_v_kernel(
         for j in range(1, PACK):
             mask_and_shift(j)
             finish_dm(j - 1, every_sample)
+            if PAIRS and j == 2:
+                for b in range(B):
+                    lay_pair(nc.scalar.copy, 0, b)
             second_mean(j)
 
         w_grouped = keep.tile([P, NC, PACK], BF16, name="w_grouped", align_bytes=64)
@@ -120,23 +193,29 @@ def tile_block_height_reducing_filtering_pb_v_kernel(
             in_=w_grouped[:].rearrange("p c j -> p (c j)"),
         )
 
-        dm_grouped = [
-            keep.tile([P, D, PACK], BF16, name="dm_grouped%d" % b, align_bytes=64) for b in range(B)
-        ]
         dm_codes = keep.tile([P, B, D], U32, name="dm_codes", align_bytes=64)
         dm_scales = keep.tile([P, B, D], U8, name="dm_scales", align_bytes=64)
 
+        def regroup(b):
+            if PAIRS:
+                lay_pair(nc.vector.tensor_copy, 2, b)
+            else:
+                dm_from, dm_to = regrouped(dm_planar[:, :, b, :], dm_grouped[:, b])
+                if b in ACT_REGROUP:
+                    nc.scalar.copy(out=dm_to, in_=dm_from)
+                else:
+                    nc.vector.tensor_copy(out=dm_to, in_=dm_from)
+
         finish_dm(last, slice(0, 1))
         for b in range(B):
-            dm_from, dm_to = regrouped(dm_planar[:, b], dm_grouped[b][:])
-            nc.vector.tensor_copy(out=dm_to, in_=dm_from)
+            regroup(b)
             if b + 1 < B:
                 finish_dm(last, slice(b + 1, b + 2))
             nc.vector.quantize_mx(
                 out=dm_codes[:, b, :].bitcast(E5M2X4), scales=dm_scales[:, b, :],
-                in_=dm_grouped[b][:].rearrange("p d j -> p (d j)"),
+                in_=dm_grouped[:, b].rearrange("p d j -> p (d j)"),
             )
-            result = ring.tile([P, HEADS, D], F32, name="result")
+            result = res_pool.tile([P, HEADS, D], F32, name="result")
             for n in range(HEADS):
                 head = slice(n * P, (n + 1) * P)
                 acc = psum.tile([P, D], F32, name="acc")
@@ -146,7 +225,7 @@ def tile_block_height_reducing_filtering_pb_v_kernel(
                     rhs=dm_codes[:, b, :].bitcast(E5M2X4), rhs_scale=dm_scales[:, b, :],
                     start=True, stop=True,
                 )
-                if b == B - 1 and n % 2 == 1:
+                if (b, n) in V_EVAC:
                     nc.vector.tensor_copy(out=result[:, n, :], in_=acc[:])
                 else:
                     nc.scalar.copy(out=result[:, n, :], in_=acc[:])

@@ -32,8 +32,11 @@ PAIRS = False
 W_AFTER = 'end'
 V_EVAC = ((3, 1), (3, 3))
 ACT_REGROUP = ()
-RESULT_BUFS = 2
-SHIFT_BUFS = 2
+RESULT_BUFS = 4
+SHIFT_BUFS = 3
+SHIFT_PARTS = {0: 1, 1: 1, 2: 1, 3: 1}
+W_TEXT = 4
+W_PLAIN = False
 
 
 def regrouped(planar, grouped):
@@ -140,10 +143,11 @@ def tile_block_height_reducing_filtering_pb_v_kernel(
                         scale=neg_a_mean[:, slot], accum_out=neg_a_s1[:, slot],
                     )
             shifted[j] = shift_pool.tile([P, B, D], F32, name="shifted")
-            nc.scalar.activation(
-                out=shifted[j][:], in_=dy_sb[j][:], func=ACT.Identity,
-                bias=neg_a_s1[:, slot], scale=a_fac[:, slot],
-            )
+            for s in pieces(SHIFT_PARTS[j]):
+                nc.scalar.activation(
+                    out=shifted[j][:, s, :], in_=dy_sb[j][:, s, :], func=ACT.Identity,
+                    bias=neg_a_s1[:, slot], scale=a_fac[:, slot],
+                )
 
         def second_mean(j):
             slot = slice(j, j + 1)
@@ -171,11 +175,32 @@ def tile_block_height_reducing_filtering_pb_v_kernel(
                 in_=dm_planar[:, first : first + 2, b, :].rearrange("p j d -> p d j"),
             )
 
+        w_grouped = keep.tile([P, NC, PACK], BF16, name="w_grouped", align_bytes=64)
+        w_codes = keep.tile([P, NC], U32, name="w_codes", align_bytes=64)
+        w_scales = keep.tile([P, NC], U8, name="w_scales", align_bytes=64)
+
+        def prepare_w():
+            if W_PLAIN:
+                nc.scalar.copy(out=w_grouped[:], in_=w_raw[:].rearrange("p j c -> p c j"))
+            else:
+                w_from, w_to = regrouped(w_raw[:], w_grouped[:])
+                nc.scalar.copy(out=w_to, in_=w_from)
+
+        def quantise_w():
+            nc.vector.quantize_mx(
+                out=w_codes[:].bitcast(E4M3X4), scales=w_scales[:],
+                in_=w_grouped[:].rearrange("p c j -> p (c j)"),
+            )
+
         every_sample = slice(0, B)
         last = PACK - 1
+        if W_TEXT == 0:
+            prepare_w()
         mask_and_shift(0)
         second_mean(0)
         for j in range(1, PACK):
+            if W_TEXT == j:
+                prepare_w()
             mask_and_shift(j)
             finish_dm(j - 1, every_sample)
             if PAIRS and j == 2:
@@ -183,15 +208,9 @@ def tile_block_height_reducing_filtering_pb_v_kernel(
                     lay_pair(nc.scalar.copy, 0, b)
             second_mean(j)
 
-        w_grouped = keep.tile([P, NC, PACK], BF16, name="w_grouped", align_bytes=64)
-        w_codes = keep.tile([P, NC], U32, name="w_codes", align_bytes=64)
-        w_scales = keep.tile([P, NC], U8, name="w_scales", align_bytes=64)
-        w_from, w_to = regrouped(w_raw[:], w_grouped[:])
-        nc.scalar.copy(out=w_to, in_=w_from)
-        nc.vector.quantize_mx(
-            out=w_codes[:].bitcast(E4M3X4), scales=w_scales[:],
-            in_=w_grouped[:].rearrange("p c j -> p (c j)"),
-        )
+        if W_TEXT == PACK:
+            prepare_w()
+        quantise_w()
 
         dm_codes = keep.tile([P, B, D], U32, name="dm_codes", align_bytes=64)
         dm_scales = keep.tile([P, B, D], U8, name="dm_scales", align_bytes=64)
@@ -206,11 +225,17 @@ def tile_block_height_reducing_filtering_pb_v_kernel(
                 else:
                     nc.vector.tensor_copy(out=dm_to, in_=dm_from)
 
-        finish_dm(last, slice(0, 1))
-        for b in range(B):
+        mine = [b for b in range(B) if b not in ACT_REGROUP]
+        finish_dm(last, slice(mine[0], mine[0] + 1))
+        for b in ACT_REGROUP:
+            finish_dm(last, slice(b, b + 1))
             regroup(b)
-            if b + 1 < B:
-                finish_dm(last, slice(b + 1, b + 2))
+        for b in range(B):
+            if b in mine:
+                regroup(b)
+                if mine.index(b) + 1 < len(mine):
+                    following = mine[mine.index(b) + 1]
+                    finish_dm(last, slice(following, following + 1))
             nc.vector.quantize_mx(
                 out=dm_codes[:, b, :].bitcast(E5M2X4), scales=dm_scales[:, b, :],
                 in_=dm_grouped[:, b].rearrange("p d j -> p (d j)"),

@@ -1,6 +1,7 @@
 from contextlib import ExitStack
 
 import concourse.mybir as mybir
+from concourse.masks import make_identity
 
 F32 = mybir.dt.float32
 BF16 = mybir.dt.bfloat16
@@ -25,18 +26,9 @@ RUN = 4
 FLOPS = 2 * CO * NC * TOKENS
 BYTES = 3 * 4 * CO * TOKENS + 2 * CO * TOKENS + 2 * CO * NC + 6 * CO
 
-MASK_PARTS = {0: 4, 1: 1, 2: 1, 3: 1}
-PROD_PARTS = {0: 4, 1: 1, 2: 1, 3: 1}
-SIGN_SLOTS = (2,)
-PAIRS = False
-W_AFTER = 'end'
 V_EVAC = ((3, 1), (3, 3))
-ACT_REGROUP = ()
-RESULT_BUFS = 4
-SHIFT_BUFS = 3
-SHIFT_PARTS = {0: 1, 1: 1, 2: 1, 3: 1}
-W_TEXT = 4
-W_PLAIN = False
+PSUM_BUFS = 7
+SIGN_SLOT = 2
 
 
 def regrouped(planar, grouped):
@@ -46,212 +38,277 @@ def regrouped(planar, grouped):
     )
 
 
-def pieces(n):
-    step = B // n
-    return [slice(k * step, (k + 1) * step) for k in range(n)]
-
-
 def tile_block_height_reducing_filtering_pb_v_kernel(
     tc, head_res, W_merge, g_m, b_m, xhat, rstd, y, grad_out, out
 ):
     nc = tc.nc
     with ExitStack() as ctx:
         keep = ctx.enter_context(tc.tile_pool(name="keep", bufs=1))
-        ring = ctx.enter_context(tc.tile_pool(name="ring", bufs=2))
-        shift_pool = ctx.enter_context(tc.tile_pool(name="shift_pool", bufs=SHIFT_BUFS))
-        res_pool = ctx.enter_context(tc.tile_pool(name="res_pool", bufs=RESULT_BUFS))
-        psum = ctx.enter_context(tc.psum_pool(name="psum", bufs=8))
+        res_pool = ctx.enter_context(tc.tile_pool(name="res_pool", bufs=4))
+        psum = ctx.enter_context(tc.psum_pool(name="psum", bufs=PSUM_BUFS))
+        sum_psum = ctx.enter_context(tc.psum_pool(name="sum_psum", bufs=1))
 
+        hbm = {
+            "g": grad_out.rearrange("b (p j) d -> j p b d", j=PACK),
+            "y": y.rearrange("b (p j) d -> j p b d", j=PACK),
+            "x": xhat.rearrange("b (p j) d -> j p b d", j=PACK),
+        }
+        sb = {
+            "g": [keep.tile([P, B, D], BF16, name="g%d" % j) for j in range(PACK)],
+            "y": [keep.tile([P, B, D], F32, name="y%d" % j) for j in range(PACK)],
+            "x": [keep.tile([P, B, D], F32, name="x%d" % j) for j in range(PACK)],
+        }
         gain_bf = keep.tile([P, PACK], BF16, name="gain_bf")
         inv_std = keep.tile([P, PACK], F32, name="inv_std")
-        nc.scalar.dma_start(out=gain_bf[:], in_=g_m.rearrange("(p j) -> p j", j=PACK))
-        nc.scalar.dma_start(out=inv_std[:], in_=rstd.rearrange("(p j) -> p j", j=PACK))
-
-        g_slots = grad_out.rearrange("b (p j) d -> j p b d", j=PACK)
-        y_slots = y.rearrange("b (p j) d -> j p b d", j=PACK)
-        x_slots = xhat.rearrange("b (p j) d -> j p b d", j=PACK)
-        g_sb = [keep.tile([P, B, D], BF16, name="g%d" % j) for j in range(PACK)]
-        y_sb = [keep.tile([P, B, D], F32, name="y%d" % j) for j in range(PACK)]
-        x_sb = [keep.tile([P, B, D], F32, name="x%d" % j) for j in range(PACK)]
         w_raw = keep.tile([P, PACK, NC], BF16, name="w_raw")
+        gain = keep.tile([P, PACK], F32, name="gain")
+        a_fac = keep.tile([P, PACK], F32, name="a_fac")
+        neg_a_mean = keep.tile([P, PACK], F32, name="neg_a_mean")
+        sum_parts = keep.tile([P, PACK, B], F32, name="sum_parts")
+        s2_parts = keep.tile([P, PACK, B], F32, name="s2_parts")
+        small_junk = keep.tile([P, PACK, B], F32, name="small_junk")
+        small_junk2 = keep.tile([P, PACK, B], F32, name="small_junk2")
+        neg_a_s1 = keep.tile([P, PACK], F32, name="neg_a_s1")
+        neg_a_s2 = keep.tile([P, PACK], F32, name="neg_a_s2")
+        dy_sb = [keep.tile([P, B, D], BF16, name="dy%d" % j) for j in range(PACK)]
+        relu_sb = [keep.tile([P, B, D], BF16, name="mask%d" % j) for j in range(PACK)]
+        shifted = [keep.tile([P, B, D], F32, name="shifted%d" % j) for j in range(PACK)]
+        products = keep.tile([P, B, D], BF16, name="products")
+        big_junk = keep.tile([P, B, D], BF16, name="big_junk")
+        dm_planar = keep.tile([P, PACK, B, D], BF16, name="dm_planar")
+        dm_grouped = keep.tile([P, B, D, PACK], BF16, name="dm_grouped", align_bytes=64)
+        w_grouped = keep.tile([P, NC, PACK], BF16, name="w_grouped", align_bytes=64)
+        w_codes = keep.tile([P, NC], U32, name="w_codes", align_bytes=64)
+        w_scales = keep.tile([P, NC], U8, name="w_scales", align_bytes=64)
+        dm_codes = keep.tile([P, B, D], U32, name="dm_codes", align_bytes=64)
+        dm_scales = keep.tile([P, B, D], U8, name="dm_scales", align_bytes=64)
+        ident = keep.tile([P, P], BF16, name="ident")
+        results = {}
+        banks = {}
+        sums = {}
+
+        def col(t, j):
+            return t[:, j : j + 1]
+
+        def sl(t):
+            a, n = t
+            return slice(a, a + n)
+
+        def load(name, j, s):
+            nc.sync.dma_start(out=sb[name][j][:, sl(s), :], in_=hbm[name][j][:, sl(s), :])
 
         def load_w():
             nc.sync.dma_start(out=w_raw[:], in_=W_merge.rearrange("(p j) c -> p j c", j=PACK))
 
-        if W_AFTER == "start":
-            load_w()
-        for j in range(PACK):
-            for s in pieces(MASK_PARTS[j]):
-                if j in SIGN_SLOTS:
-                    nc.sync.dma_start(out=y_sb[j][:, s, :], in_=y_slots[j][:, s, :])
-                    nc.sync.dma_start(out=g_sb[j][:, s, :], in_=g_slots[j][:, s, :])
-                else:
-                    nc.sync.dma_start(out=g_sb[j][:, s, :], in_=g_slots[j][:, s, :])
-                    nc.sync.dma_start(out=y_sb[j][:, s, :], in_=y_slots[j][:, s, :])
-            if W_AFTER == ("y", j):
-                load_w()
-            for s in pieces(PROD_PARTS[j]):
-                nc.sync.dma_start(out=x_sb[j][:, s, :], in_=x_slots[j][:, s, :])
-            if W_AFTER == ("x", j):
-                load_w()
-        if W_AFTER == "end":
-            load_w()
+        def load_small():
+            nc.scalar.dma_start(out=gain_bf[:], in_=g_m.rearrange("(p j) -> p j", j=PACK))
+            nc.scalar.dma_start(out=inv_std[:], in_=rstd.rearrange("(p j) -> p j", j=PACK))
 
-        gain = keep.tile([P, PACK], F32, name="gain")
-        a_fac = keep.tile([P, PACK], F32, name="a_fac")
-        neg_a_mean = keep.tile([P, PACK], F32, name="neg_a_mean")
-        nc.vector.tensor_copy(out=gain[:], in_=gain_bf[:])
-        nc.vector.tensor_mul(out=a_fac[:], in0=gain[:], in1=inv_std[:])
-        nc.vector.tensor_scalar_mul(out=neg_a_mean[:], in0=a_fac[:], scalar1=-1.0 / TOKENS)
+        def factors():
+            nc.gpsimd.tensor_copy(out=gain[:], in_=gain_bf[:])
+            nc.gpsimd.tensor_mul(out=a_fac[:], in0=gain[:], in1=inv_std[:])
+            nc.gpsimd.tensor_scalar(out=neg_a_mean[:], in0=a_fac[:], scalar1=-1.0 / TOKENS, scalar2=0.0, op0=ALU.mult, op1=ALU.add)
 
-        sum_parts = keep.tile([P, PACK, B], F32, name="sum_parts")
-        s2_parts = keep.tile([P, PACK, B], F32, name="s2_parts")
-        small_junk = keep.tile([P, PACK, B], F32, name="small_junk")
-        neg_a_s1 = keep.tile([P, PACK], F32, name="neg_a_s1")
-        neg_a_s2 = keep.tile([P, PACK], F32, name="neg_a_s2")
-        dy_sb = [keep.tile([P, B, D], BF16, name="dy%d" % j) for j in range(PACK)]
-        shifted = {}
-        dm_planar = keep.tile([P, PACK, B, D], BF16, name="dm_planar")
-        dm_grouped = keep.tile([P, B, D, PACK], BF16, name="dm_grouped", align_bytes=64)
+        def identity():
+            make_identity(nc, ident[:])
 
-        def mask_and_shift(j):
-            slot = slice(j, j + 1)
-            n = MASK_PARTS[j]
-            if j in SIGN_SLOTS:
-                for s in pieces(n):
-                    relu_mask = ring.tile([P, B, D], BF16, name="relu_mask")
-                    nc.scalar.activation(out=relu_mask[:, s, :], in_=y_sb[j][:, s, :], func=ACT.Sign)
-                    nc.vector.tensor_tensor(
-                        out=dy_sb[j][:, s, :], in0=relu_mask[:, s, :], in1=g_sb[j][:, s, :], op=ALU.mult
-                    )
-                big_junk = keep.tile([P, B, D], BF16, name="big_junk")
-                nc.scalar.activation(
-                    out=big_junk[:], in_=dy_sb[j][:], func=ACT.Copy,
-                    scale=neg_a_mean[:, slot], accum_out=neg_a_s1[:, slot],
-                )
-            else:
-                for k, s in enumerate(pieces(n)):
-                    nc.vector.scalar_tensor_tensor(
-                        out=dy_sb[j][:, s, :], in0=y_sb[j][:, s, :], scalar=0.0, in1=g_sb[j][:, s, :],
-                        op0=ALU.is_gt, op1=ALU.mult, accum_out=sum_parts[:, j, k : k + 1],
-                    )
-                if n == 1:
-                    nc.scalar.mul(out=neg_a_s1[:, slot], in_=sum_parts[:, j, 0:1], mul=neg_a_mean[:, slot])
-                else:
-                    nc.scalar.activation(
-                        out=small_junk[:, j, 0:n], in_=sum_parts[:, j, 0:n], func=ACT.Copy,
-                        scale=neg_a_mean[:, slot], accum_out=neg_a_s1[:, slot],
-                    )
-            shifted[j] = shift_pool.tile([P, B, D], F32, name="shifted")
-            for s in pieces(SHIFT_PARTS[j]):
-                nc.scalar.activation(
-                    out=shifted[j][:, s, :], in_=dy_sb[j][:, s, :], func=ACT.Identity,
-                    bias=neg_a_s1[:, slot], scale=a_fac[:, slot],
-                )
+        def warm_table():
+            warm = keep.tile([P, 1], F32, name="warm")
+            nc.gpsimd.memset(warm[:], 0.0)
+            nc.scalar.activation(out=warm[:], in_=warm[:], func=ACT.Identity)
 
-        def second_mean(j):
-            slot = slice(j, j + 1)
-            n = PROD_PARTS[j]
-            products = keep.tile([P, B, D], BF16, name="products")
-            for k, s in enumerate(pieces(n)):
-                nc.vector.scalar_tensor_tensor(
-                    out=products[:, s, :], in0=dy_sb[j][:, s, :], scalar=neg_a_mean[:, slot],
-                    in1=x_sb[j][:, s, :], op0=ALU.mult, op1=ALU.mult,
-                    accum_out=(neg_a_s2[:, slot] if n == 1 else s2_parts[:, j, k : k + 1]),
-                )
-            if n > 1:
-                nc.vector.tensor_reduce(out=neg_a_s2[:, slot], in_=s2_parts[:, j, 0:n], axis=AX.X, op=ALU.add)
+        def sign(j, s):
+            nc.scalar.activation(out=relu_sb[j][:, sl(s), :], in_=sb["y"][j][:, sl(s), :], func=ACT.Sign)
 
-        def finish_dm(j, samples):
+        def mask(j, k, s):
             nc.vector.scalar_tensor_tensor(
-                out=dm_planar[:, j, samples, :], in0=x_sb[j][:, samples, :],
-                scalar=neg_a_s2[:, j : j + 1], in1=shifted[j][:, samples, :],
-                op0=ALU.mult, op1=ALU.add,
+                out=dy_sb[j][:, sl(s), :], in0=sb["y"][j][:, sl(s), :], scalar=0.0, in1=sb["g"][j][:, sl(s), :],
+                op0=ALU.is_gt, op1=ALU.mult, accum_out=sum_parts[:, j, k : k + 1],
             )
 
-        def lay_pair(engine_copy, first, b):
-            engine_copy(
+        def mask_by_sign(j, s):
+            nc.vector.tensor_tensor(
+                out=dy_sb[j][:, sl(s), :], in0=relu_sb[j][:, sl(s), :], in1=sb["g"][j][:, sl(s), :], op=ALU.mult
+            )
+
+        def sum_of_parts(j, n):
+            if n == 1:
+                nc.scalar.mul(out=col(neg_a_s1, j), in_=sum_parts[:, j, 0:1], mul=col(neg_a_mean, j))
+            else:
+                nc.scalar.activation(
+                    out=small_junk[:, j, 0:n], in_=sum_parts[:, j, 0:n], func=ACT.Copy,
+                    scale=col(neg_a_mean, j), accum_out=col(neg_a_s1, j),
+                )
+
+        def sum_by_scalar(j):
+            nc.scalar.activation(
+                out=big_junk[:], in_=dy_sb[j][:], func=ACT.Copy, scale=col(neg_a_mean, j), accum_out=col(neg_a_s1, j)
+            )
+
+        def sum_by_tensor(j, s):
+            a, n = s
+            if j not in sums:
+                sums[j] = sum_psum.tile([P, D], F32, name="sum_acc")
+            for b in range(a, a + n):
+                nc.tensor.matmul(out=sums[j][:], lhsT=ident[:], rhs=dy_sb[j][:, b, :], start=(b == 0), stop=(b == B - 1))
+
+        def sum_from_bank(j):
+            nc.scalar.activation(
+                out=big_junk[:, 0, :], in_=sums[j][:], func=ACT.Copy, scale=col(neg_a_mean, j), accum_out=col(neg_a_s1, j)
+            )
+
+        def bracket(j, s):
+            nc.scalar.activation(
+                out=shifted[j][:, sl(s), :], in_=dy_sb[j][:, sl(s), :], func=ACT.Identity,
+                bias=col(neg_a_s1, j), scale=col(a_fac, j),
+            )
+
+        def product(j, k, s):
+            whole = s == (0, B)
+            nc.vector.scalar_tensor_tensor(
+                out=products[:, sl(s), :], in0=dy_sb[j][:, sl(s), :], scalar=col(neg_a_mean, j),
+                in1=sb["x"][j][:, sl(s), :], op0=ALU.mult, op1=ALU.mult,
+                accum_out=(col(neg_a_s2, j) if whole else s2_parts[:, j, k : k + 1]),
+            )
+
+        def second_sum(j, n):
+            nc.scalar.activation(
+                out=small_junk2[:, j, 0:n], in_=s2_parts[:, j, 0:n], func=ACT.Copy, accum_out=col(neg_a_s2, j)
+            )
+
+        def finish(j, s):
+            nc.vector.scalar_tensor_tensor(
+                out=dm_planar[:, j, sl(s), :], in0=sb["x"][j][:, sl(s), :], scalar=col(neg_a_s2, j),
+                in1=shifted[j][:, sl(s), :], op0=ALU.mult, op1=ALU.add,
+            )
+
+        def lay_pair(copy, first, b):
+            copy(
                 out=dm_grouped[:, b, :, first : first + 2],
                 in_=dm_planar[:, first : first + 2, b, :].rearrange("p j d -> p d j"),
             )
 
-        w_grouped = keep.tile([P, NC, PACK], BF16, name="w_grouped", align_bytes=64)
-        w_codes = keep.tile([P, NC], U32, name="w_codes", align_bytes=64)
-        w_scales = keep.tile([P, NC], U8, name="w_scales", align_bytes=64)
+        def pair01(b):
+            lay_pair(nc.scalar.copy, 0, b)
+
+        def pair23(b):
+            lay_pair(nc.vector.tensor_copy, 2, b)
+
+        def regroup(b):
+            dm_from, dm_to = regrouped(dm_planar[:, :, b, :], dm_grouped[:, b])
+            nc.vector.tensor_copy(out=dm_to, in_=dm_from)
+
+        def regroup_s(b):
+            dm_from, dm_to = regrouped(dm_planar[:, :, b, :], dm_grouped[:, b])
+            nc.scalar.copy(out=dm_to, in_=dm_from)
 
         def prepare_w():
-            if W_PLAIN:
-                nc.scalar.copy(out=w_grouped[:], in_=w_raw[:].rearrange("p j c -> p c j"))
-            else:
-                w_from, w_to = regrouped(w_raw[:], w_grouped[:])
-                nc.scalar.copy(out=w_to, in_=w_from)
+            w_from, w_to = regrouped(w_raw[:], w_grouped[:])
+            nc.scalar.copy(out=w_to, in_=w_from)
 
         def quantise_w():
             nc.vector.quantize_mx(
-                out=w_codes[:].bitcast(E4M3X4), scales=w_scales[:],
-                in_=w_grouped[:].rearrange("p c j -> p (c j)"),
+                out=w_codes[:].bitcast(E4M3X4), scales=w_scales[:], in_=w_grouped[:].rearrange("p c j -> p (c j)")
             )
 
-        every_sample = slice(0, B)
-        last = PACK - 1
-        if W_TEXT == 0:
-            prepare_w()
-        mask_and_shift(0)
-        second_mean(0)
-        for j in range(1, PACK):
-            if W_TEXT == j:
-                prepare_w()
-            mask_and_shift(j)
-            finish_dm(j - 1, every_sample)
-            if PAIRS and j == 2:
-                for b in range(B):
-                    lay_pair(nc.scalar.copy, 0, b)
-            second_mean(j)
-
-        if W_TEXT == PACK:
-            prepare_w()
-        quantise_w()
-
-        dm_codes = keep.tile([P, B, D], U32, name="dm_codes", align_bytes=64)
-        dm_scales = keep.tile([P, B, D], U8, name="dm_scales", align_bytes=64)
-
-        def regroup(b):
-            if PAIRS:
-                lay_pair(nc.vector.tensor_copy, 2, b)
-            else:
-                dm_from, dm_to = regrouped(dm_planar[:, :, b, :], dm_grouped[:, b])
-                if b in ACT_REGROUP:
-                    nc.scalar.copy(out=dm_to, in_=dm_from)
-                else:
-                    nc.vector.tensor_copy(out=dm_to, in_=dm_from)
-
-        mine = [b for b in range(B) if b not in ACT_REGROUP]
-        finish_dm(last, slice(mine[0], mine[0] + 1))
-        for b in ACT_REGROUP:
-            finish_dm(last, slice(b, b + 1))
-            regroup(b)
-        for b in range(B):
-            if b in mine:
-                regroup(b)
-                if mine.index(b) + 1 < len(mine):
-                    following = mine[mine.index(b) + 1]
-                    finish_dm(last, slice(following, following + 1))
+        def quantise(b):
             nc.vector.quantize_mx(
                 out=dm_codes[:, b, :].bitcast(E5M2X4), scales=dm_scales[:, b, :],
                 in_=dm_grouped[:, b].rearrange("p d j -> p (d j)"),
             )
-            result = res_pool.tile([P, HEADS, D], F32, name="result")
+
+        def multiply(b, n):
+            head = slice(n * P, (n + 1) * P)
+            banks[b, n] = psum.tile([P, D], F32, name="acc")
+            nc.tensor.matmul_mx(
+                out=banks[b, n][:],
+                lhsT=w_codes[:, head].bitcast(E4M3X4), lhsT_scale=w_scales[:, head],
+                rhs=dm_codes[:, b, :].bitcast(E5M2X4), rhs_scale=dm_scales[:, b, :],
+                start=True, stop=True,
+            )
+
+        def empty(b, n):
+            if b not in results:
+                results[b] = res_pool.tile([P, HEADS, D], F32, name="result")
+            if (b, n) in V_EVAC:
+                nc.vector.tensor_copy(out=results[b][:, n, :], in_=banks[b, n][:])
+            else:
+                nc.scalar.copy(out=results[b][:, n, :], in_=banks[b, n][:])
+
+        def store(b, n):
+            nc.sync.dma_start(out=out[n, b], in_=results[b][:, n, :])
+
+        WHOLE = (0, B)
+
+        def deliver(b):
             for n in range(HEADS):
-                head = slice(n * P, (n + 1) * P)
-                acc = psum.tile([P, D], F32, name="acc")
-                nc.tensor.matmul_mx(
-                    out=acc[:],
-                    lhsT=w_codes[:, head].bitcast(E4M3X4), lhsT_scale=w_scales[:, head],
-                    rhs=dm_codes[:, b, :].bitcast(E5M2X4), rhs_scale=dm_scales[:, b, :],
-                    start=True, stop=True,
-                )
-                if (b, n) in V_EVAC:
-                    nc.vector.tensor_copy(out=result[:, n, :], in_=acc[:])
-                else:
-                    nc.scalar.copy(out=result[:, n, :], in_=acc[:])
-                nc.sync.dma_start(out=out[n, b], in_=result[:, n, :])
+                multiply(b, n)
+                empty(b, n)
+                store(b, n)
+
+        with tc.manual_schedule():
+            identity()
+            warm_table()
+            load_small()
+            factors()
+            for b in range(B):
+                load("g", 0, (b, 1))
+                load("y", 0, (b, 1))
+            for b in range(B):
+                load("x", 0, (b, 1))
+            load_w()
+            for j in range(1, PACK):
+                for name in ("y", "g", "x") if j == SIGN_SLOT else ("g", "y", "x"):
+                    load(name, j, WHOLE)
+
+            for b in range(B):
+                mask(0, b, (b, 1))
+            sum_of_parts(0, B)
+            bracket(0, WHOLE)
+            for b in range(B):
+                product(0, b, (b, 1))
+            second_sum(0, B)
+            prepare_w()
+            finish(0, WHOLE)
+
+            mask(1, 0, WHOLE)
+            sum_of_parts(1, 1)
+            bracket(1, WHOLE)
+            product(1, 0, WHOLE)
+            sign(2, WHOLE)
+            finish(1, WHOLE)
+
+            mask_by_sign(2, WHOLE)
+            sum_by_tensor(2, WHOLE)
+            quantise_w()
+            pair01(0)
+            sum_from_bank(2)
+            bracket(2, WHOLE)
+            product(2, 0, WHOLE)
+            pair01(1)
+
+            mask(3, 0, WHOLE)
+            sum_of_parts(3, 1)
+            bracket(3, (0, 1))
+            bracket(3, (1, 1))
+            pair01(2)
+            bracket(3, (2, 1))
+            bracket(3, (3, 1))
+            pair01(3)
+            product(3, 0, WHOLE)
+
+            finish(2, (0, 1))
+            finish(3, (0, 1))
+            finish(2, (1, 1))
+            pair23(0)
+            finish(3, (1, 1))
+            quantise(0)
+            for b in range(1, B):
+                if b + 1 < B:
+                    finish(2, (b + 1, 1))
+                pair23(b)
+                if b + 1 < B:
+                    finish(3, (b + 1, 1))
+                quantise(b)
+            for b in range(B):
+                deliver(b)

@@ -247,10 +247,10 @@ def tile_block_height_reducing_filtering_pb_v_kernel(
                 store(b, n)
 
         with tc.manual_schedule():
-            identity()
-            warm_table()
             load_small()
+            warm_table()
             factors()
+            identity()
             for b in range(B):
                 load("g", 0, (b, 1))
                 load("y", 0, (b, 1))

@@ -28,7 +28,6 @@ BYTES = 3 * 4 * CO * TOKENS + 2 * CO * TOKENS + 2 * CO * NC + 6 * CO
 
 V_EVAC = ((3, 1), (3, 3))
 PSUM_BUFS = 7
-SIGN_SLOT = 2
 
 
 def regrouped(planar, grouped):
@@ -239,6 +238,8 @@ def tile_block_height_reducing_filtering_pb_v_kernel(
             nc.sync.dma_start(out=out[n, b], in_=results[b][:, n, :])
 
         WHOLE = (0, B)
+        HALVES = ((0, 2), (2, 2))
+        FIRST = ((0, 1), (1, 1), (2, 2))
 
         def deliver(b):
             for n in range(HEADS):
@@ -251,23 +252,30 @@ def tile_block_height_reducing_filtering_pb_v_kernel(
             warm_table()
             factors()
             identity()
-            for b in range(B):
-                load("g", 0, (b, 1))
-                load("y", 0, (b, 1))
-            for b in range(B):
-                load("x", 0, (b, 1))
+            for s in FIRST:
+                load("g", 0, s)
+                load("y", 0, s)
+            for s in HALVES:
+                load("x", 0, s)
+            load("g", 1, WHOLE)
+            load("y", 1, WHOLE)
             load_w()
-            for j in range(1, PACK):
-                for name in ("y", "g", "x") if j == SIGN_SLOT else ("g", "y", "x"):
-                    load(name, j, WHOLE)
+            load("x", 1, WHOLE)
+            for name in ("y", "g", "x"):
+                load(name, 2, WHOLE)
+            for s in HALVES:
+                load("g", 3, s)
+                load("y", 3, s)
+            for s in HALVES:
+                load("x", 3, s)
 
-            for b in range(B):
-                mask(0, b, (b, 1))
-            sum_of_parts(0, B)
+            for k, s in enumerate(FIRST):
+                mask(0, k, s)
+            sum_of_parts(0, len(FIRST))
             bracket(0, WHOLE)
-            for b in range(B):
-                product(0, b, (b, 1))
-            second_sum(0, B)
+            for k, s in enumerate(HALVES):
+                product(0, k, s)
+            second_sum(0, 2)
             prepare_w()
             finish(0, WHOLE)
 
@@ -275,27 +283,30 @@ def tile_block_height_reducing_filtering_pb_v_kernel(
             sum_of_parts(1, 1)
             bracket(1, WHOLE)
             product(1, 0, WHOLE)
+            quantise_w()
             sign(2, WHOLE)
             finish(1, WHOLE)
 
             mask_by_sign(2, WHOLE)
             sum_by_tensor(2, WHOLE)
-            quantise_w()
             pair01(0)
             sum_from_bank(2)
             bracket(2, WHOLE)
             product(2, 0, WHOLE)
             pair01(1)
 
-            mask(3, 0, WHOLE)
-            sum_of_parts(3, 1)
+            for k, s in enumerate(HALVES):
+                mask(3, k, s)
+            sum_of_parts(3, 2)
             bracket(3, (0, 1))
             bracket(3, (1, 1))
+            for k, s in enumerate(HALVES):
+                product(3, k, s)
+            second_sum(3, 2)
             pair01(2)
             bracket(3, (2, 1))
             bracket(3, (3, 1))
             pair01(3)
-            product(3, 0, WHOLE)
 
             finish(2, (0, 1))
             finish(3, (0, 1))

@@ -93,8 +93,8 @@ def tile_block_height_reducing_filtering_pb_v_kernel(
             a, n = t
             return slice(a, a + n)
 
-        def load(name, j, s):
-            nc.sync.dma_start(out=sb[name][j][:, sl(s), :], in_=hbm[name][j][:, sl(s), :])
+        def load(name, j, s, queue=nc.sync):
+            queue.dma_start(out=sb[name][j][:, sl(s), :], in_=hbm[name][j][:, sl(s), :])
 
         def load_w():
             nc.sync.dma_start(out=w_raw[:], in_=W_merge.rearrange("(p j) c -> p j c", j=PACK))
@@ -191,7 +191,10 @@ def tile_block_height_reducing_filtering_pb_v_kernel(
             lay_pair(nc.scalar.copy, 0, b)
 
         def pair23(b):
-            lay_pair(nc.vector.tensor_copy, 2, b)
+            nc.vector.tensor_copy(
+                out=dm_grouped[:, b, :, 2:4].rearrange("p (c i) j -> p c j i", i=RUN),
+                in_=dm_planar[:, 2:4, b, :].rearrange("p j (c i) -> p c j i", i=RUN),
+            )
 
         def regroup(b):
             dm_from, dm_to = regrouped(dm_planar[:, :, b, :], dm_grouped[:, b])

@@ -74,7 +74,7 @@ def tile_block_height_reducing_filtering_pb_v_kernel(
         shifted = [keep.tile([P, B, D], F32, name="shifted%d" % j) for j in range(PACK)]
         products = keep.tile([P, B, D], BF16, name="products")
         big_junk = keep.tile([P, B, D], BF16, name="big_junk")
-        dm_planar = keep.tile([P, PACK, B, D], BF16, name="dm_planar")
+        dm_planar = keep.tile([P, B, PACK, D], BF16, name="dm_planar")
         dm_grouped = keep.tile([P, B, D, PACK], BF16, name="dm_grouped", align_bytes=64)
         w_grouped = keep.tile([P, NC, PACK], BF16, name="w_grouped", align_bytes=64)
         w_codes = keep.tile([P, NC], U32, name="w_codes", align_bytes=64)
@@ -177,14 +177,14 @@ def tile_block_height_reducing_filtering_pb_v_kernel(
 
         def finish(j, s):
             nc.vector.scalar_tensor_tensor(
-                out=dm_planar[:, j, sl(s), :], in0=sb["x"][j][:, sl(s), :], scalar=col(neg_a_s2, j),
+                out=dm_planar[:, sl(s), j, :], in0=sb["x"][j][:, sl(s), :], scalar=col(neg_a_s2, j),
                 in1=shifted[j][:, sl(s), :], op0=ALU.mult, op1=ALU.add,
             )
 
         def lay_pair(copy, first, b):
             copy(
                 out=dm_grouped[:, b, :, first : first + 2],
-                in_=dm_planar[:, first : first + 2, b, :].rearrange("p j d -> p d j"),
+                in_=dm_planar[:, b, first : first + 2, :].rearrange("p j d -> p d j"),
             )
 
         def pair01(b):
@@ -193,15 +193,15 @@ def tile_block_height_reducing_filtering_pb_v_kernel(
         def pair23(b):
             nc.vector.tensor_copy(
                 out=dm_grouped[:, b, :, 2:4].rearrange("p (c i) j -> p c j i", i=RUN),
-                in_=dm_planar[:, 2:4, b, :].rearrange("p j (c i) -> p c j i", i=RUN),
+                in_=dm_planar[:, b, 2:4, :].rearrange("p j (c i) -> p c j i", i=RUN),
             )
 
         def regroup(b):
-            dm_from, dm_to = regrouped(dm_planar[:, :, b, :], dm_grouped[:, b])
+            dm_from, dm_to = regrouped(dm_planar[:, b], dm_grouped[:, b])
             nc.vector.tensor_copy(out=dm_to, in_=dm_from)
 
         def regroup_s(b):
-            dm_from, dm_to = regrouped(dm_planar[:, :, b, :], dm_grouped[:, b])
+            dm_from, dm_to = regrouped(dm_planar[:, b], dm_grouped[:, b])
             nc.scalar.copy(out=dm_to, in_=dm_from)
 
         def prepare_w():

from contextlib import ExitStack

import concourse.mybir as mybir
from concourse.masks import make_identity

F32 = mybir.dt.float32
BF16 = mybir.dt.bfloat16
U32 = mybir.dt.uint32
U8 = mybir.dt.uint8
E4M3X4 = mybir.dt.float8_e4m3fn_x4
E5M2X4 = mybir.dt.float8_e5m2_x4
ALU = mybir.AluOpType
ACT = mybir.ActivationFunctionType
AX = mybir.AxisListType

P = 128
PACK = 4
B = 4
D = 512
HEADS = 4
CO = P * PACK
NC = HEADS * P
TOKENS = B * D
RUN = 4

FLOPS = 2 * CO * NC * TOKENS
BYTES = 3 * 4 * CO * TOKENS + 2 * CO * TOKENS + 2 * CO * NC + 6 * CO

V_EVAC = ((3, 1), (3, 3))
PSUM_BUFS = 7


def regrouped(planar, grouped):
    return (
        planar.rearrange("p j (c i) -> p c j i", i=RUN),
        grouped.rearrange("p (c i) j -> p c j i", i=RUN),
    )


def tile_block_height_reducing_filtering_pb_v_kernel(
    tc, head_res, W_merge, g_m, b_m, xhat, rstd, y, grad_out, out
):
    nc = tc.nc
    with ExitStack() as ctx:
        keep = ctx.enter_context(tc.tile_pool(name="keep", bufs=1))
        res_pool = ctx.enter_context(tc.tile_pool(name="res_pool", bufs=4))
        psum = ctx.enter_context(tc.psum_pool(name="psum", bufs=PSUM_BUFS))
        sum_psum = ctx.enter_context(tc.psum_pool(name="sum_psum", bufs=1))

        hbm = {
            "g": grad_out.rearrange("b (p j) d -> j p b d", j=PACK),
            "y": y.rearrange("b (p j) d -> j p b d", j=PACK),
            "x": xhat.rearrange("b (p j) d -> j p b d", j=PACK),
        }
        sb = {
            "g": [keep.tile([P, B, D], BF16, name="g%d" % j) for j in range(PACK)],
            "y": [keep.tile([P, B, D], F32, name="y%d" % j) for j in range(PACK)],
            "x": [keep.tile([P, B, D], F32, name="x%d" % j) for j in range(PACK)],
        }
        gain_bf = keep.tile([P, PACK], BF16, name="gain_bf")
        inv_std = keep.tile([P, PACK], F32, name="inv_std")
        w_raw = keep.tile([P, PACK, NC], BF16, name="w_raw")
        gain = keep.tile([P, PACK], F32, name="gain")
        a_fac = keep.tile([P, PACK], F32, name="a_fac")
        neg_a_mean = keep.tile([P, PACK], F32, name="neg_a_mean")
        sum_parts = keep.tile([P, PACK, B], F32, name="sum_parts")
        s2_parts = keep.tile([P, PACK, B], F32, name="s2_parts")
        small_junk = keep.tile([P, PACK, B], F32, name="small_junk")
        small_junk2 = keep.tile([P, PACK, B], F32, name="small_junk2")
        neg_a_s1 = keep.tile([P, PACK], F32, name="neg_a_s1")
        neg_a_s2 = keep.tile([P, PACK], F32, name="neg_a_s2")
        dy_sb = [keep.tile([P, B, D], BF16, name="dy%d" % j) for j in range(PACK)]
        relu_sb = [keep.tile([P, B, D], BF16, name="mask%d" % j) for j in range(PACK)]
        shifted = [keep.tile([P, B, D], F32, name="shifted%d" % j) for j in range(PACK)]
        products = keep.tile([P, B, D], BF16, name="products")
        big_junk = keep.tile([P, B, D], BF16, name="big_junk")
        dm_planar = keep.tile([P, B, PACK, D], BF16, name="dm_planar")
        dm_grouped = keep.tile([P, B, D, PACK], BF16, name="dm_grouped", align_bytes=64)
        w_grouped = keep.tile([P, NC, PACK], BF16, name="w_grouped", align_bytes=64)
        w_codes = keep.tile([P, NC], U32, name="w_codes", align_bytes=64)
        w_scales = keep.tile([P, NC], U8, name="w_scales", align_bytes=64)
        dm_codes = keep.tile([P, B, D], U32, name="dm_codes", align_bytes=64)
        dm_scales = keep.tile([P, B, D], U8, name="dm_scales", align_bytes=64)
        ident = keep.tile([P, P], BF16, name="ident")
        results = {}
        banks = {}
        sums = {}

        def col(t, j):
            return t[:, j : j + 1]

        def sl(t):
            a, n = t
            return slice(a, a + n)

        def load(name, j, s, queue=nc.sync):
            queue.dma_start(out=sb[name][j][:, sl(s), :], in_=hbm[name][j][:, sl(s), :])

        def load_w():
            nc.sync.dma_start(out=w_raw[:], in_=W_merge.rearrange("(p j) c -> p j c", j=PACK))

        def load_small():
            nc.scalar.dma_start(out=gain_bf[:], in_=g_m.rearrange("(p j) -> p j", j=PACK))
            nc.scalar.dma_start(out=inv_std[:], in_=rstd.rearrange("(p j) -> p j", j=PACK))

        def factors():
            nc.gpsimd.tensor_copy(out=gain[:], in_=gain_bf[:])
            nc.gpsimd.tensor_mul(out=a_fac[:], in0=gain[:], in1=inv_std[:])
            nc.gpsimd.tensor_scalar(out=neg_a_mean[:], in0=a_fac[:], scalar1=-1.0 / TOKENS, scalar2=0.0, op0=ALU.mult, op1=ALU.add)

        def identity():
            make_identity(nc, ident[:])

        def warm_table():
            warm = keep.tile([P, 1], F32, name="warm")
            nc.gpsimd.memset(warm[:], 0.0)
            nc.scalar.activation(out=warm[:], in_=warm[:], func=ACT.Identity)

        def sign(j, s):
            nc.scalar.activation(out=relu_sb[j][:, sl(s), :], in_=sb["y"][j][:, sl(s), :], func=ACT.Sign)

        def mask(j, k, s):
            nc.vector.scalar_tensor_tensor(
                out=dy_sb[j][:, sl(s), :], in0=sb["y"][j][:, sl(s), :], scalar=0.0, in1=sb["g"][j][:, sl(s), :],
                op0=ALU.is_gt, op1=ALU.mult, accum_out=sum_parts[:, j, k : k + 1],
            )

        def mask_by_sign(j, s):
            nc.vector.tensor_tensor(
                out=dy_sb[j][:, sl(s), :], in0=relu_sb[j][:, sl(s), :], in1=sb["g"][j][:, sl(s), :], op=ALU.mult
            )

        def sum_of_parts(j, n):
            if n == 1:
                nc.scalar.mul(out=col(neg_a_s1, j), in_=sum_parts[:, j, 0:1], mul=col(neg_a_mean, j))
            else:
                nc.scalar.activation(
                    out=small_junk[:, j, 0:n], in_=sum_parts[:, j, 0:n], func=ACT.Copy,
                    scale=col(neg_a_mean, j), accum_out=col(neg_a_s1, j),
                )

        def sum_by_scalar(j):
            nc.scalar.activation(
                out=big_junk[:], in_=dy_sb[j][:], func=ACT.Copy, scale=col(neg_a_mean, j), accum_out=col(neg_a_s1, j)
            )

        def sum_by_tensor(j, s):
            a, n = s
            if j not in sums:
                sums[j] = sum_psum.tile([P, D], F32, name="sum_acc")
            for b in range(a, a + n):
                nc.tensor.matmul(out=sums[j][:], lhsT=ident[:], rhs=dy_sb[j][:, b, :], start=(b == 0), stop=(b == B - 1))

        def sum_from_bank(j):
            nc.scalar.activation(
                out=big_junk[:, 0, :], in_=sums[j][:], func=ACT.Copy, scale=col(neg_a_mean, j), accum_out=col(neg_a_s1, j)
            )

        def bracket(j, s):
            nc.scalar.activation(
                out=shifted[j][:, sl(s), :], in_=dy_sb[j][:, sl(s), :], func=ACT.Identity,
                bias=col(neg_a_s1, j), scale=col(a_fac, j),
            )

        def product(j, k, s):
            whole = s == (0, B)
            nc.vector.scalar_tensor_tensor(
                out=products[:, sl(s), :], in0=dy_sb[j][:, sl(s), :], scalar=col(neg_a_mean, j),
                in1=sb["x"][j][:, sl(s), :], op0=ALU.mult, op1=ALU.mult,
                accum_out=(col(neg_a_s2, j) if whole else s2_parts[:, j, k : k + 1]),
            )

        def second_sum(j, n):
            nc.scalar.activation(
                out=small_junk2[:, j, 0:n], in_=s2_parts[:, j, 0:n], func=ACT.Copy, accum_out=col(neg_a_s2, j)
            )

        def finish(j, s):
            nc.vector.scalar_tensor_tensor(
                out=dm_planar[:, sl(s), j, :], in0=sb["x"][j][:, sl(s), :], scalar=col(neg_a_s2, j),
                in1=shifted[j][:, sl(s), :], op0=ALU.mult, op1=ALU.add,
            )

        def lay_pair(copy, first, b):
            copy(
                out=dm_grouped[:, b, :, first : first + 2],
                in_=dm_planar[:, b, first : first + 2, :].rearrange("p j d -> p d j"),
            )

        def pair01(b):
            lay_pair(nc.scalar.copy, 0, b)

        def pair23(b):
            nc.vector.tensor_copy(
                out=dm_grouped[:, b, :, 2:4].rearrange("p (c i) j -> p c j i", i=RUN),
                in_=dm_planar[:, b, 2:4, :].rearrange("p j (c i) -> p c j i", i=RUN),
            )

        def regroup(b):
            dm_from, dm_to = regrouped(dm_planar[:, b], dm_grouped[:, b])
            nc.vector.tensor_copy(out=dm_to, in_=dm_from)

        def regroup_s(b):
            dm_from, dm_to = regrouped(dm_planar[:, b], dm_grouped[:, b])
            nc.scalar.copy(out=dm_to, in_=dm_from)

        def prepare_w():
            w_from, w_to = regrouped(w_raw[:], w_grouped[:])
            nc.scalar.copy(out=w_to, in_=w_from)

        def quantise_w():
            nc.vector.quantize_mx(
                out=w_codes[:].bitcast(E4M3X4), scales=w_scales[:], in_=w_grouped[:].rearrange("p c j -> p (c j)")
            )

        def quantise(b):
            nc.vector.quantize_mx(
                out=dm_codes[:, b, :].bitcast(E5M2X4), scales=dm_scales[:, b, :],
                in_=dm_grouped[:, b].rearrange("p d j -> p (d j)"),
            )

        def multiply(b, n):
            head = slice(n * P, (n + 1) * P)
            banks[b, n] = psum.tile([P, D], F32, name="acc")
            nc.tensor.matmul_mx(
                out=banks[b, n][:],
                lhsT=w_codes[:, head].bitcast(E4M3X4), lhsT_scale=w_scales[:, head],
                rhs=dm_codes[:, b, :].bitcast(E5M2X4), rhs_scale=dm_scales[:, b, :],
                start=True, stop=True,
            )

        def empty(b, n):
            if b not in results:
                results[b] = res_pool.tile([P, HEADS, D], F32, name="result")
            if (b, n) in V_EVAC:
                nc.vector.tensor_copy(out=results[b][:, n, :], in_=banks[b, n][:])
            else:
                nc.scalar.copy(out=results[b][:, n, :], in_=banks[b, n][:])

        def store(b, n):
            nc.sync.dma_start(out=out[n, b], in_=results[b][:, n, :])

        WHOLE = (0, B)
        HALVES = ((0, 2), (2, 2))
        FIRST = ((0, 1), (1, 1), (2, 2))

        def deliver(b):
            for n in range(HEADS):
                multiply(b, n)
                empty(b, n)
                store(b, n)

        with tc.manual_schedule():
            load_small()
            warm_table()
            factors()
            identity()
            for s in FIRST:
                load("g", 0, s)
                load("y", 0, s)
            for s in HALVES:
                load("x", 0, s)
            load("g", 1, WHOLE)
            load("y", 1, WHOLE)
            load_w()
            load("x", 1, WHOLE)
            for name in ("y", "g", "x"):
                load(name, 2, WHOLE)
            for s in HALVES:
                load("g", 3, s)
                load("y", 3, s)
            for s in HALVES:
                load("x", 3, s)

            for k, s in enumerate(FIRST):
                mask(0, k, s)
            sum_of_parts(0, len(FIRST))
            bracket(0, WHOLE)
            for k, s in enumerate(HALVES):
                product(0, k, s)
            second_sum(0, 2)
            prepare_w()
            finish(0, WHOLE)

            mask(1, 0, WHOLE)
            sum_of_parts(1, 1)
            bracket(1, WHOLE)
            product(1, 0, WHOLE)
            quantise_w()
            sign(2, WHOLE)
            finish(1, WHOLE)

            mask_by_sign(2, WHOLE)
            sum_by_tensor(2, WHOLE)
            pair01(0)
            sum_from_bank(2)
            bracket(2, WHOLE)
            product(2, 0, WHOLE)
            pair01(1)

            for k, s in enumerate(HALVES):
                mask(3, k, s)
            sum_of_parts(3, 2)
            bracket(3, (0, 1))
            bracket(3, (1, 1))
            for k, s in enumerate(HALVES):
                product(3, k, s)
            second_sum(3, 2)
            pair01(2)
            bracket(3, (2, 1))
            bracket(3, (3, 1))
            pair01(3)

            finish(2, (0, 1))
            finish(3, (0, 1))
            finish(2, (1, 1))
            pair23(0)
            finish(3, (1, 1))
            quantise(0)
            for b in range(1, B):
                if b + 1 < B:
                    finish(2, (b + 1, 1))
                pair23(b)
                if b + 1 < B:
                    finish(3, (b + 1, 1))
                quantise(b)
            for b in range(B):
                deliver(b)
